import numpy as np
import ml_dtypes


def mxq(x, axis, fmt="e4m3"):
    dtype, down = {"e4m3": (ml_dtypes.float8_e4m3fn, 7), "e5m2": (ml_dtypes.float8_e5m2, 14)}[fmt]
    v = np.moveaxis(np.asarray(x, np.float32).astype(ml_dtypes.bfloat16).astype(np.float64), axis, -1)
    blocks = v.reshape(v.shape[:-1] + (-1, 32))
    amax = np.abs(blocks).max(-1, keepdims=True)
    byte = np.maximum(np.where(amax > 0, np.frexp(amax)[1] - 1 + 127, 0) - down, 1)
    scale = np.exp2(byte - 127.0)
    codes = (blocks / scale).astype(np.float32).astype(dtype).astype(np.float64)
    return np.moveaxis((codes * scale).reshape(v.shape), -1, axis)


WIDE = False


def mx_kscale(k):
    if not WIDE:
        return np.ones(k)
    levels = np.array([10, -10, 5, -5, 0])
    if k % 512:
        return np.exp2(np.random.permutation(np.resize(levels, k // 32))).repeat(32)
    a = np.empty((k // 512, 16))
    for p in range(k // 512):
        a[p, :8] = np.random.permutation(np.resize(levels, 8))
        for g in range(8):
            far = levels[np.abs(levels - a[p, g]) >= 10]
            a[p, g + 8] = far[np.random.randint(len(far))]
    return np.exp2(a.ravel()).repeat(32)


BF16 = ml_dtypes.bfloat16


def bf(x):
    return np.asarray(x, np.float32).astype(BF16)


def f64(x):
    return np.asarray(x).astype(np.float64)


B, IMG, P0, P1, C, F = 2, 256, 8, 16, 2, 512
E0, E1 = IMG // P0, IMG // P1
N0, N1 = E0 * E0, E1 * E1
D0, D1 = P0 * P0 * C, P1 * P1 * C


def setup_inputs():
    s = mx_kscale(D1)
    flat = np.random.standard_normal((B, N1, D1)) * s
    img = flat.reshape(B, E1, E1, P1, P1, C).transpose(0, 1, 3, 2, 4, 5).reshape(B, IMG, IMG, C)
    encoded = img.reshape(B, E0, P0, E0, P0, C).transpose(0, 1, 3, 2, 4, 5).reshape(B, N0, D0)
    return {"encoded": bf(encoded),
            "W": bf(np.random.standard_normal((D1, F)) / np.sqrt(D1) / s[:, None]),
            "b": bf(np.random.standard_normal(F) * 0.3),
            "pos_emb": bf(np.random.standard_normal((N1, F)) * 0.5)}


def reference(encoded, W, b, pos_emb):
    x = f64(encoded).reshape(-1, E0, E0, P0, P0, C)
    img = x.transpose(0, 1, 3, 2, 4, 5).reshape(-1, IMG, IMG, C)
    new_patches = img.reshape(-1, E1, P1, E1, P1, C).transpose(0, 1, 3, 2, 4, 5)
    flat = new_patches.reshape(-1, N1, D1)
    return (mxq(flat, 2, "e4m3") @ mxq(f64(W), 0, "e4m3")) + f64(b) + f64(pos_emb)

@@ -1,0 +1,148 @@
+from contextlib import ExitStack
+
+import concourse.mybir as mybir
+from concourse.masks import make_identity
+
+BF16 = mybir.dt.bfloat16
+F32 = mybir.dt.float32
+U32 = mybir.dt.uint32
+U8 = mybir.dt.uint8
+FP8X4 = mybir.dt.float8_e4m3fn_x4
+ADD = mybir.AluOpType.add
+
+P = 128
+PACK = 4
+IMAGES = 2
+TOKENS = 512
+K = 512
+F = 512
+TOKEN_TILES = TOKENS // P
+TILES_PER_IMAGE = TOKEN_TILES // IMAGES
+
+W_PARTS = 2
+PART = F // W_PARTS
+VECTOR_COLS = 344
+FLOPS = 2 * TOKENS * K * F
+
+
+def tile_resampling_s_kernel(tc, encoded, W, b, pos_emb, out):
+    nc = tc.nc
+    with ExitStack() as ctx:
+        keep = ctx.enter_context(tc.tile_pool(name="keep", bufs=1))
+        psum = ctx.enter_context(tc.psum_pool(name="psum", bufs=1))
+        ctx.enter_context(tc.manual_schedule())
+
+        ident = keep.tile([P, P], F32)
+        ones = keep.tile([P, P], BF16)
+        b_row = keep.tile([1, F], BF16)
+        b_rows = keep.tile([P, F], BF16)
+        x_raw = [keep.tile([P, 2, 512], BF16, name="x_raw%d" % i) for i in range(IMAGES)]
+        x_ord = [keep.tile([P, 4, 2, 128], BF16, name="x_ord%d" % i) for i in range(IMAGES)]
+        xt = [psum.tile([P, TILES_PER_IMAGE, 2, P], F32, name="xt%d" % i) for i in range(IMAGES)]
+        x_cols = TILES_PER_IMAGE * P
+        x_grp = [keep.tile([P, x_cols * PACK], BF16, name="x_grp%d" % i, align_bytes=64) for i in range(IMAGES)]
+        x_codes = [keep.tile([P, x_cols], U32, name="x_codes%d" % i, align_bytes=64) for i in range(IMAGES)]
+        x_scales = [keep.tile([P, x_cols], U8, name="x_scales%d" % i, align_bytes=64) for i in range(IMAGES)]
+        pos_sb = keep.tile([P, TILES_PER_IMAGE, F], BF16)
+        bias_ps = psum.tile([P, F], F32)
+        posb = keep.tile([P, TILES_PER_IMAGE, F], F32)
+        w_raw = keep.tile([P, PACK, F], BF16)
+        w_grp = [keep.tile([P, PART, PACK], BF16, name="w_grp%d" % c, align_bytes=64) for c in range(W_PARTS)]
+        w_codes = [keep.tile([P, PART], U32, name="w_codes%d" % c, align_bytes=64) for c in range(W_PARTS)]
+        w_scales = [keep.tile([P, PART], U8, name="w_scales%d" % c, align_bytes=64) for c in range(W_PARTS)]
+
+        patches = encoded.rearrange("i (gy rh gx q) d -> i rh gy gx (q d)", gy=16, rh=2, gx=8)
+
+        def load_x(i, rh):
+            nc.sync.dma_start(out=x_raw[i][:, rh, :], in_=patches[i, rh])
+
+        def reorder_x(i, rh):
+            nc.vector.tensor_copy(
+                out=x_ord[i][:, :, rh, :], in_=x_raw[i][:, rh, :].rearrange("p (q d) -> p q d", q=4)
+            )
+
+        def transpose_x(i):
+            for h in range(TILES_PER_IMAGE):
+                for c in range(2):
+                    words = x_ord[i][:, 2 * h + c, :, :].rearrange("p r d -> p (r d)").bitcast(F32)
+                    nc.tensor.transpose(xt[i][:, h, c, :], words, ident[:])
+
+        def group_x(i):
+            nc.scalar.copy(
+                out=x_grp[i][:].bitcast(F32).rearrange("p (h n c) -> p h n c", h=2, c=2),
+                in_=xt[i][:].rearrange("p h c n -> p h n c"),
+            )
+
+        def quantise_x(i):
+            nc.vector.quantize_mx(out=x_codes[i][:].bitcast(FP8X4), scales=x_scales[i][:], in_=x_grp[i][:])
+
+        def add_b_to_pos(h):
+            nc.vector.tensor_tensor(out=posb[:, h, :], in0=bias_ps[:], in1=pos_sb[:, h, :], op=ADD)
+
+        def regroup_columns(copy, c, lo, hi):
+            copy(
+                out=w_grp[c][:, lo - c * PART : hi - c * PART, :].rearrange("p (a i) t -> p a t i", i=4),
+                in_=w_raw[:, :, lo:hi].rearrange("p t (a i) -> p a t i", i=4),
+            )
+
+        def regroup_w(c):
+            split = min(max(VECTOR_COLS, c * PART), (c + 1) * PART)
+            if split > c * PART:
+                regroup_columns(nc.vector.tensor_copy, c, c * PART, split)
+            if split < (c + 1) * PART:
+                regroup_columns(nc.scalar.copy, c, split, (c + 1) * PART)
+
+        def quantise_w(c):
+            nc.vector.quantize_mx(
+                out=w_codes[c][:].bitcast(FP8X4),
+                scales=w_scales[c][:],
+                in_=w_grp[c][:].rearrange("p n t -> p (n t)"),
+            )
+
+        def project(c, i):
+            cols = slice(c * PART, (c + 1) * PART)
+            acc = psum.tile([P, TILES_PER_IMAGE, PART], F32, name="acc%d%d" % (c, i))
+            for h in range(TILES_PER_IMAGE):
+                tokens = slice(h * P, (h + 1) * P)
+                nc.tensor.matmul_mx(
+                    out=acc[:, h, :],
+                    lhsT=x_codes[i][:, tokens].bitcast(FP8X4),
+                    lhsT_scale=x_scales[i][:, tokens],
+                    rhs=w_codes[c][:].bitcast(FP8X4),
+                    rhs_scale=w_scales[c][:],
+                    start=True,
+                    stop=True,
+                )
+            res = keep.tile([P, TILES_PER_IMAGE, PART], F32, name="res%d%d" % (c, i))
+            nc.vector.tensor_tensor(out=res[:], in0=acc[:], in1=posb[:, :, cols], op=ADD)
+            nc.sync.dma_start(out=out[i].rearrange("(p h) n -> p h n", h=TILES_PER_IMAGE)[:, :, cols], in_=res[:])
+
+        nc.sync.dma_start(out=b_row[:], in_=b.unsqueeze(0))
+        nc.vector.memset(b_rows[:], 0.0)
+        nc.vector.memset(ones[:], 1.0)
+        make_identity(nc, ident[:])
+        load_x(0, 0)
+        load_x(0, 1)
+        nc.sync.dma_start(out=pos_sb[:], in_=pos_emb.rearrange("(p h) n -> p h n", h=TILES_PER_IMAGE))
+        load_x(1, 0)
+        load_x(1, 1)
+        w_rows = W.rearrange("(g c x e) n -> c g x (e n)", g=16, c=2, x=8)
+        for c in range(2):
+            nc.sync.dma_start(out=w_raw[:, 2 * c : 2 * c + 2, :].rearrange("p e n -> p (e n)"), in_=w_rows[c])
+
+        nc.vector.tensor_copy(out=b_rows[0:1, :], in_=b_row[:])
+        nc.tensor.matmul(out=bias_ps[:], lhsT=ones[:], rhs=b_rows[:], start=True, stop=True)
+        for i in range(IMAGES):
+            reorder_x(i, 0)
+            reorder_x(i, 1)
+            transpose_x(i)
+            group_x(i)
+            add_b_to_pos(i)
+        for c in range(W_PARTS):
+            quantise_x(c)
+            regroup_w(c)
+            quantise_w(c)
+
+        for c in range(W_PARTS):
+            for i in range(IMAGES):
+                project(c, i)

@@ -37,7 +37,7 @@ def tile_resampling_s_kernel(tc, encoded, W, b, pos_emb, out):
         b_row = keep.tile([1, F], BF16)
         b_rows = keep.tile([P, F], BF16)
         x_raw = [keep.tile([P, 2, 512], BF16, name="x_raw%d" % i) for i in range(IMAGES)]
-        x_ord = [keep.tile([P, 4, 2, 128], BF16, name="x_ord%d" % i) for i in range(IMAGES)]
+        x_ord = [keep.tile([P, 2, 2, 256], BF16, name="x_ord%d" % i) for i in range(IMAGES)]
         xt = [psum.tile([P, TILES_PER_IMAGE, 2, P], F32, name="xt%d" % i) for i in range(IMAGES)]
         x_cols = TILES_PER_IMAGE * P
         x_grp = [keep.tile([P, x_cols * PACK], BF16, name="x_grp%d" % i, align_bytes=64) for i in range(IMAGES)]
@@ -58,19 +58,20 @@ def tile_resampling_s_kernel(tc, encoded, W, b, pos_emb, out):
 
         def reorder_x(i, rh):
             nc.vector.tensor_copy(
-                out=x_ord[i][:, :, rh, :], in_=x_raw[i][:, rh, :].rearrange("p (q d) -> p q d", q=4)
+                out=x_ord[i][:, :, rh, :].rearrange("p h (r c e) -> p h r c e", r=8, c=2),
+                in_=x_raw[i][:, rh, :].rearrange("p (h c r e) -> p h r c e", h=2, c=2, r=8),
             )
 
         def transpose_x(i):
             for h in range(TILES_PER_IMAGE):
-                for c in range(2):
-                    words = x_ord[i][:, 2 * h + c, :, :].rearrange("p r d -> p (r d)").bitcast(F32)
-                    nc.tensor.transpose(xt[i][:, h, c, :], words, ident[:])
+                words = x_ord[i][:, h, :, :].rearrange("p r e -> p (r e)").bitcast(F32)
+                for w in range(2):
+                    nc.tensor.transpose(xt[i][:, h, w, :], words[:, w::2], ident[:])
 
         def group_x(i):
             nc.scalar.copy(
-                out=x_grp[i][:].bitcast(F32).rearrange("p (h n c) -> p h n c", h=2, c=2),
-                in_=xt[i][:].rearrange("p h c n -> p h n c"),
+                out=x_grp[i][:].bitcast(F32).rearrange("p (h n w) -> p h n w", h=2, w=2),
+                in_=xt[i][:].rearrange("p h w n -> p h n w"),
             )
 
         def quantise_x(i):
@@ -126,9 +127,7 @@ def tile_resampling_s_kernel(tc, encoded, W, b, pos_emb, out):
         nc.sync.dma_start(out=pos_sb[:], in_=pos_emb.rearrange("(p h) n -> p h n", h=TILES_PER_IMAGE))
         load_x(1, 0)
         load_x(1, 1)
-        w_rows = W.rearrange("(g c x e) n -> c g x (e n)", g=16, c=2, x=8)
-        for c in range(2):
-            nc.sync.dma_start(out=w_raw[:, 2 * c : 2 * c + 2, :].rearrange("p e n -> p (e n)"), in_=w_rows[c])
+        nc.sync.dma_start(out=w_raw[:], in_=W.rearrange("(p t) n -> p t n", t=PACK))
 
         nc.vector.tensor_copy(out=b_rows[0:1, :], in_=b_row[:])
         nc.tensor.matmul(out=bias_ps[:], lhsT=ones[:], rhs=b_rows[:], start=True, stop=True)

@@ -135,13 +135,16 @@ def tile_resampling_s_kernel(tc, encoded, W, b, pos_emb, out):
             reorder_x(i, 0)
             reorder_x(i, 1)
             transpose_x(i)
-            group_x(i)
             add_b_to_pos(i)
-        for c in range(W_PARTS):
-            quantise_x(c)
-            regroup_w(c)
-            quantise_w(c)
+        group_x(0)
+        regroup_w(0)
+        quantise_x(0)
+        regroup_w(1)
+        group_x(1)
+        quantise_w(0)
+        quantise_w(1)
+        quantise_x(1)
 
-        for c in range(W_PARTS):
-            for i in range(IMAGES):
+        for i in range(IMAGES):
+            for c in range(W_PARTS):
                 project(c, i)

@@ -21,7 +21,7 @@ TILES_PER_IMAGE = TOKEN_TILES // IMAGES
 
 W_PARTS = 2
 PART = F // W_PARTS
-VECTOR_COLS = 344
+VECTOR_COLS = 176
 FLOPS = 2 * TOKENS * K * F
 
 
@@ -46,7 +46,7 @@ def tile_resampling_s_kernel(tc, encoded, W, b, pos_emb, out):
         pos_sb = keep.tile([P, TILES_PER_IMAGE, F], BF16)
         bias_ps = psum.tile([P, F], F32)
         posb = keep.tile([P, TILES_PER_IMAGE, F], F32)
-        w_raw = keep.tile([P, PACK, F], BF16)
+        w_raw = [keep.tile([P, PACK, PART], BF16, name="w_raw%d" % c) for c in range(W_PARTS)]
         w_grp = [keep.tile([P, PART, PACK], BF16, name="w_grp%d" % c, align_bytes=64) for c in range(W_PARTS)]
         w_codes = [keep.tile([P, PART], U32, name="w_codes%d" % c, align_bytes=64) for c in range(W_PARTS)]
         w_scales = [keep.tile([P, PART], U8, name="w_scales%d" % c, align_bytes=64) for c in range(W_PARTS)]
@@ -82,16 +82,13 @@ def tile_resampling_s_kernel(tc, encoded, W, b, pos_emb, out):
 
         def regroup_columns(copy, c, lo, hi):
             copy(
-                out=w_grp[c][:, lo - c * PART : hi - c * PART, :].rearrange("p (a i) t -> p a t i", i=4),
-                in_=w_raw[:, :, lo:hi].rearrange("p t (a i) -> p a t i", i=4),
+                out=w_grp[c][:, lo:hi, :].rearrange("p (a i) t -> p a t i", i=4),
+                in_=w_raw[c][:, :, lo:hi].rearrange("p t (a i) -> p a t i", i=4),
             )
 
         def regroup_w(c):
-            split = min(max(VECTOR_COLS, c * PART), (c + 1) * PART)
-            if split > c * PART:
-                regroup_columns(nc.vector.tensor_copy, c, c * PART, split)
-            if split < (c + 1) * PART:
-                regroup_columns(nc.scalar.copy, c, split, (c + 1) * PART)
+            regroup_columns(nc.vector.tensor_copy, c, 0, VECTOR_COLS)
+            regroup_columns(nc.scalar.copy, c, VECTOR_COLS, PART)
 
         def quantise_w(c):
             nc.vector.quantize_mx(
@@ -127,7 +124,10 @@ def tile_resampling_s_kernel(tc, encoded, W, b, pos_emb, out):
         nc.sync.dma_start(out=pos_sb[:], in_=pos_emb.rearrange("(p h) n -> p h n", h=TILES_PER_IMAGE))
         load_x(1, 0)
         load_x(1, 1)
-        nc.sync.dma_start(out=w_raw[:], in_=W.rearrange("(p t) n -> p t n", t=PACK))
+        for c in range(W_PARTS):
+            nc.sync.dma_start(
+                out=w_raw[c][:], in_=W.rearrange("(p t) n -> p t n", t=PACK)[:, :, c * PART : (c + 1) * PART]
+            )
 
         nc.vector.tensor_copy(out=b_rows[0:1, :], in_=b_row[:])
         nc.tensor.matmul(out=bias_ps[:], lhsT=ones[:], rhs=b_rows[:], start=True, stop=True)
@@ -139,12 +139,12 @@ def tile_resampling_s_kernel(tc, encoded, W, b, pos_emb, out):
         group_x(0)
         regroup_w(0)
         quantise_x(0)
+        quantise_w(0)
         regroup_w(1)
         group_x(1)
-        quantise_w(0)
-        quantise_w(1)
         quantise_x(1)
+        quantise_w(1)
 
-        for i in range(IMAGES):
-            for c in range(W_PARTS):
+        for c in range(W_PARTS):
+            for i in range(IMAGES):
                 project(c, i)

@@ -37,7 +37,7 @@ def tile_resampling_s_kernel(tc, encoded, W, b, pos_emb, out):
         b_row = keep.tile([1, F], BF16)
         b_rows = keep.tile([P, F], BF16)
         x_raw = [keep.tile([P, 2, 512], BF16, name="x_raw%d" % i) for i in range(IMAGES)]
-        x_ord = [keep.tile([P, 2, 2, 256], BF16, name="x_ord%d" % i) for i in range(IMAGES)]
+        x_ord = [keep.tile([P, 2, 2, 2, 64], F32, name="x_ord%d" % i) for i in range(IMAGES)]
         xt = [psum.tile([P, TILES_PER_IMAGE, 2, P], F32, name="xt%d" % i) for i in range(IMAGES)]
         x_cols = TILES_PER_IMAGE * P
         x_grp = [keep.tile([P, x_cols * PACK], BF16, name="x_grp%d" % i, align_bytes=64) for i in range(IMAGES)]
@@ -45,6 +45,7 @@ def tile_resampling_s_kernel(tc, encoded, W, b, pos_emb, out):
         x_scales = [keep.tile([P, x_cols], U8, name="x_scales%d" % i, align_bytes=64) for i in range(IMAGES)]
         pos_sb = keep.tile([P, TILES_PER_IMAGE, F], BF16)
         bias_ps = psum.tile([P, F], F32)
+        spare = psum.tile([P, 4, P], F32)
         posb = keep.tile([P, TILES_PER_IMAGE, F], F32)
         w_raw = [keep.tile([P, PACK, PART], BF16, name="w_raw%d" % c) for c in range(W_PARTS)]
         w_grp = [keep.tile([P, PART, PACK], BF16, name="w_grp%d" % c, align_bytes=64) for c in range(W_PARTS)]
@@ -56,17 +57,21 @@ def tile_resampling_s_kernel(tc, encoded, W, b, pos_emb, out):
         def load_x(i, rh):
             nc.sync.dma_start(out=x_raw[i][:, rh, :], in_=patches[i, rh])
 
-        def reorder_x(i, rh):
-            nc.vector.tensor_copy(
-                out=x_ord[i][:, :, rh, :].rearrange("p h (r c e) -> p h r c e", r=8, c=2),
-                in_=x_raw[i][:, rh, :].rearrange("p (h c r e) -> p h r c e", h=2, c=2, r=8),
+        def reorder_x(copy, i, rh, w):
+            copy(
+                out=x_ord[i][:, :, w, rh, :].rearrange("p h (r c j) -> p h r c j", r=8, c=2),
+                in_=x_raw[i][:, rh, :].bitcast(F32).rearrange("p (h c r j w) -> p w h r c j", h=2, c=2, r=8, w=2)[:, w],
             )
 
         def transpose_x(i):
             for h in range(TILES_PER_IMAGE):
-                words = x_ord[i][:, h, :, :].rearrange("p r e -> p (r e)").bitcast(F32)
                 for w in range(2):
-                    nc.tensor.transpose(xt[i][:, h, w, :], words[:, w::2], ident[:])
+                    words = x_ord[i][:, h, w, :, :].rearrange("p r m -> p (r m)")
+                    nc.tensor.transpose(xt[i][:, h, w, :], words, ident[:])
+
+        def keep_clock(n):
+            for k in range(n):
+                nc.tensor.transpose(spare[:, k % 4, :], ident[:], ident[:])
 
         def group_x(i):
             nc.scalar.copy(
@@ -97,13 +102,14 @@ def tile_resampling_s_kernel(tc, encoded, W, b, pos_emb, out):
                 in_=w_grp[c][:].rearrange("p n t -> p (n t)"),
             )
 
-        def project(c, i):
-            cols = slice(c * PART, (c + 1) * PART)
-            acc = psum.tile([P, TILES_PER_IMAGE, PART], F32, name="acc%d%d" % (c, i))
+        acc = {}
+
+        def multiply(c, i):
+            acc[c, i] = psum.tile([P, TILES_PER_IMAGE, PART], F32, name="acc%d%d" % (c, i))
             for h in range(TILES_PER_IMAGE):
                 tokens = slice(h * P, (h + 1) * P)
                 nc.tensor.matmul_mx(
-                    out=acc[:, h, :],
+                    out=acc[c, i][:, h, :],
                     lhsT=x_codes[i][:, tokens].bitcast(FP8X4),
                     lhsT_scale=x_scales[i][:, tokens],
                     rhs=w_codes[c][:].bitcast(FP8X4),
@@ -111,9 +117,22 @@ def tile_resampling_s_kernel(tc, encoded, W, b, pos_emb, out):
                     start=True,
                     stop=True,
                 )
+
+        def out_cols(c, i):
+            return out[i].rearrange("(p h) n -> p h n", h=TILES_PER_IMAGE)[:, :, c * PART : (c + 1) * PART]
+
+        def finish(c, i):
             res = keep.tile([P, TILES_PER_IMAGE, PART], F32, name="res%d%d" % (c, i))
-            nc.vector.tensor_tensor(out=res[:], in0=acc[:], in1=posb[:, :, cols], op=ADD)
-            nc.sync.dma_start(out=out[i].rearrange("(p h) n -> p h n", h=TILES_PER_IMAGE)[:, :, cols], in_=res[:])
+            nc.vector.tensor_tensor(out=res[:], in0=acc[c, i][:], in1=posb[:, :, c * PART : (c + 1) * PART], op=ADD)
+            nc.sync.dma_start(out=out_cols(c, i), in_=res[:])
+
+        def finish_by_halves(c, i):
+            for h in range(TILES_PER_IMAGE):
+                res = keep.tile([P, PART], F32, name="res%d%d%d" % (c, i, h))
+                nc.vector.tensor_tensor(
+                    out=res[:], in0=acc[c, i][:, h, :], in1=posb[:, h, c * PART : (c + 1) * PART], op=ADD
+                )
+                nc.sync.dma_start(out=out_cols(c, i)[:, h, :], in_=res[:])
 
         nc.sync.dma_start(out=b_row[:], in_=b.unsqueeze(0))
         nc.vector.memset(b_rows[:], 0.0)
@@ -132,19 +151,25 @@ def tile_resampling_s_kernel(tc, encoded, W, b, pos_emb, out):
         nc.vector.tensor_copy(out=b_rows[0:1, :], in_=b_row[:])
         nc.tensor.matmul(out=bias_ps[:], lhsT=ones[:], rhs=b_rows[:], start=True, stop=True)
         for i in range(IMAGES):
-            reorder_x(i, 0)
-            reorder_x(i, 1)
+            for rh in range(2):
+                reorder_x(nc.vector.tensor_copy, i, rh, 0)
+                reorder_x(nc.scalar.copy, i, rh, 1)
             transpose_x(i)
+            keep_clock(4)
             add_b_to_pos(i)
         group_x(0)
         regroup_w(0)
         quantise_x(0)
         quantise_w(0)
-        regroup_w(1)
+        multiply(0, 0)
         group_x(1)
+        regroup_w(1)
         quantise_x(1)
+        finish(0, 0)
+        multiply(0, 1)
         quantise_w(1)
-
-        for c in range(W_PARTS):
-            for i in range(IMAGES):
-                project(c, i)
+        for i in range(IMAGES):
+            multiply(1, i)
+        finish(0, 1)
+        finish(1, 0)
+        finish_by_halves(1, 1)

@@ -140,9 +140,9 @@ def tile_resampling_s_kernel(tc, encoded, W, b, pos_emb, out):
         make_identity(nc, ident[:])
         load_x(0, 0)
         load_x(0, 1)
-        nc.sync.dma_start(out=pos_sb[:], in_=pos_emb.rearrange("(p h) n -> p h n", h=TILES_PER_IMAGE))
         load_x(1, 0)
         load_x(1, 1)
+        nc.sync.dma_start(out=pos_sb[:], in_=pos_emb.rearrange("(p h) n -> p h n", h=TILES_PER_IMAGE))
         for c in range(W_PARTS):
             nc.sync.dma_start(
                 out=w_raw[c][:], in_=W.rearrange("(p t) n -> p t n", t=PACK)[:, :, c * PART : (c + 1) * PART]
@@ -156,12 +156,13 @@ def tile_resampling_s_kernel(tc, encoded, W, b, pos_emb, out):
                 reorder_x(nc.scalar.copy, i, rh, 1)
             transpose_x(i)
             keep_clock(4)
-            add_b_to_pos(i)
         group_x(0)
+        add_b_to_pos(0)
         regroup_w(0)
         quantise_x(0)
         quantise_w(0)
         multiply(0, 0)
+        add_b_to_pos(1)
         group_x(1)
         regroup_w(1)
         quantise_x(1)

from contextlib import ExitStack

import concourse.mybir as mybir
from concourse.masks import make_identity

BF16 = mybir.dt.bfloat16
F32 = mybir.dt.float32
U32 = mybir.dt.uint32
U8 = mybir.dt.uint8
FP8X4 = mybir.dt.float8_e4m3fn_x4
ADD = mybir.AluOpType.add

P = 128
PACK = 4
IMAGES = 2
TOKENS = 512
K = 512
F = 512
TOKEN_TILES = TOKENS // P
TILES_PER_IMAGE = TOKEN_TILES // IMAGES

W_PARTS = 2
PART = F // W_PARTS
VECTOR_COLS = 176
FLOPS = 2 * TOKENS * K * F


def tile_resampling_s_kernel(tc, encoded, W, b, pos_emb, out):
    nc = tc.nc
    with ExitStack() as ctx:
        keep = ctx.enter_context(tc.tile_pool(name="keep", bufs=1))
        psum = ctx.enter_context(tc.psum_pool(name="psum", bufs=1))
        ctx.enter_context(tc.manual_schedule())

        ident = keep.tile([P, P], F32)
        ones = keep.tile([P, P], BF16)
        b_row = keep.tile([1, F], BF16)
        b_rows = keep.tile([P, F], BF16)
        x_raw = [keep.tile([P, 2, 512], BF16, name="x_raw%d" % i) for i in range(IMAGES)]
        x_ord = [keep.tile([P, 2, 2, 2, 64], F32, name="x_ord%d" % i) for i in range(IMAGES)]
        xt = [psum.tile([P, TILES_PER_IMAGE, 2, P], F32, name="xt%d" % i) for i in range(IMAGES)]
        x_cols = TILES_PER_IMAGE * P
        x_grp = [keep.tile([P, x_cols * PACK], BF16, name="x_grp%d" % i, align_bytes=64) for i in range(IMAGES)]
        x_codes = [keep.tile([P, x_cols], U32, name="x_codes%d" % i, align_bytes=64) for i in range(IMAGES)]
        x_scales = [keep.tile([P, x_cols], U8, name="x_scales%d" % i, align_bytes=64) for i in range(IMAGES)]
        pos_sb = keep.tile([P, TILES_PER_IMAGE, F], BF16)
        bias_ps = psum.tile([P, F], F32)
        spare = psum.tile([P, 4, P], F32)
        posb = keep.tile([P, TILES_PER_IMAGE, F], F32)
        w_raw = [keep.tile([P, PACK, PART], BF16, name="w_raw%d" % c) for c in range(W_PARTS)]
        w_grp = [keep.tile([P, PART, PACK], BF16, name="w_grp%d" % c, align_bytes=64) for c in range(W_PARTS)]
        w_codes = [keep.tile([P, PART], U32, name="w_codes%d" % c, align_bytes=64) for c in range(W_PARTS)]
        w_scales = [keep.tile([P, PART], U8, name="w_scales%d" % c, align_bytes=64) for c in range(W_PARTS)]

        patches = encoded.rearrange("i (gy rh gx q) d -> i rh gy gx (q d)", gy=16, rh=2, gx=8)

        def load_x(i, rh):
            nc.sync.dma_start(out=x_raw[i][:, rh, :], in_=patches[i, rh])

        def reorder_x(copy, i, rh, w):
            copy(
                out=x_ord[i][:, :, w, rh, :].rearrange("p h (r c j) -> p h r c j", r=8, c=2),
                in_=x_raw[i][:, rh, :].bitcast(F32).rearrange("p (h c r j w) -> p w h r c j", h=2, c=2, r=8, w=2)[:, w],
            )

        def transpose_x(i):
            for h in range(TILES_PER_IMAGE):
                for w in range(2):
                    words = x_ord[i][:, h, w, :, :].rearrange("p r m -> p (r m)")
                    nc.tensor.transpose(xt[i][:, h, w, :], words, ident[:])

        def keep_clock(n):
            for k in range(n):
                nc.tensor.transpose(spare[:, k % 4, :], ident[:], ident[:])

        def group_x(i):
            nc.scalar.copy(
                out=x_grp[i][:].bitcast(F32).rearrange("p (h n w) -> p h n w", h=2, w=2),
                in_=xt[i][:].rearrange("p h w n -> p h n w"),
            )

        def quantise_x(i):
            nc.vector.quantize_mx(out=x_codes[i][:].bitcast(FP8X4), scales=x_scales[i][:], in_=x_grp[i][:])

        def add_b_to_pos(h):
            nc.vector.tensor_tensor(out=posb[:, h, :], in0=bias_ps[:], in1=pos_sb[:, h, :], op=ADD)

        def regroup_columns(copy, c, lo, hi):
            copy(
                out=w_grp[c][:, lo:hi, :].rearrange("p (a i) t -> p a t i", i=4),
                in_=w_raw[c][:, :, lo:hi].rearrange("p t (a i) -> p a t i", i=4),
            )

        def regroup_w(c):
            regroup_columns(nc.vector.tensor_copy, c, 0, VECTOR_COLS)
            regroup_columns(nc.scalar.copy, c, VECTOR_COLS, PART)

        def quantise_w(c):
            nc.vector.quantize_mx(
                out=w_codes[c][:].bitcast(FP8X4),
                scales=w_scales[c][:],
                in_=w_grp[c][:].rearrange("p n t -> p (n t)"),
            )

        acc = {}

        def multiply(c, i):
            acc[c, i] = psum.tile([P, TILES_PER_IMAGE, PART], F32, name="acc%d%d" % (c, i))
            for h in range(TILES_PER_IMAGE):
                tokens = slice(h * P, (h + 1) * P)
                nc.tensor.matmul_mx(
                    out=acc[c, i][:, h, :],
                    lhsT=x_codes[i][:, tokens].bitcast(FP8X4),
                    lhsT_scale=x_scales[i][:, tokens],
                    rhs=w_codes[c][:].bitcast(FP8X4),
                    rhs_scale=w_scales[c][:],
                    start=True,
                    stop=True,
                )

        def out_cols(c, i):
            return out[i].rearrange("(p h) n -> p h n", h=TILES_PER_IMAGE)[:, :, c * PART : (c + 1) * PART]

        def finish(c, i):
            res = keep.tile([P, TILES_PER_IMAGE, PART], F32, name="res%d%d" % (c, i))
            nc.vector.tensor_tensor(out=res[:], in0=acc[c, i][:], in1=posb[:, :, c * PART : (c + 1) * PART], op=ADD)
            nc.sync.dma_start(out=out_cols(c, i), in_=res[:])

        def finish_by_halves(c, i):
            for h in range(TILES_PER_IMAGE):
                res = keep.tile([P, PART], F32, name="res%d%d%d" % (c, i, h))
                nc.vector.tensor_tensor(
                    out=res[:], in0=acc[c, i][:, h, :], in1=posb[:, h, c * PART : (c + 1) * PART], op=ADD
                )
                nc.sync.dma_start(out=out_cols(c, i)[:, h, :], in_=res[:])

        nc.sync.dma_start(out=b_row[:], in_=b.unsqueeze(0))
        nc.vector.memset(b_rows[:], 0.0)
        nc.vector.memset(ones[:], 1.0)
        make_identity(nc, ident[:])
        load_x(0, 0)
        load_x(0, 1)
        load_x(1, 0)
        load_x(1, 1)
        nc.sync.dma_start(out=pos_sb[:], in_=pos_emb.rearrange("(p h) n -> p h n", h=TILES_PER_IMAGE))
        for c in range(W_PARTS):
            nc.sync.dma_start(
                out=w_raw[c][:], in_=W.rearrange("(p t) n -> p t n", t=PACK)[:, :, c * PART : (c + 1) * PART]
            )

        nc.vector.tensor_copy(out=b_rows[0:1, :], in_=b_row[:])
        nc.tensor.matmul(out=bias_ps[:], lhsT=ones[:], rhs=b_rows[:], start=True, stop=True)
        for i in range(IMAGES):
            for rh in range(2):
                reorder_x(nc.vector.tensor_copy, i, rh, 0)
                reorder_x(nc.scalar.copy, i, rh, 1)
            transpose_x(i)
            keep_clock(4)
        group_x(0)
        add_b_to_pos(0)
        regroup_w(0)
        quantise_x(0)
        quantise_w(0)
        multiply(0, 0)
        add_b_to_pos(1)
        group_x(1)
        regroup_w(1)
        quantise_x(1)
        finish(0, 0)
        multiply(0, 1)
        quantise_w(1)
        for i in range(IMAGES):
            multiply(1, i)
        finish(0, 1)
        finish(1, 0)
        finish_by_halves(1, 1)
